import numpy as np
import ml_dtypes


def mxq(x, axis, fmt="e4m3"):
    dtype, down = {"e4m3": (ml_dtypes.float8_e4m3fn, 7), "e5m2": (ml_dtypes.float8_e5m2, 14)}[fmt]
    v = np.moveaxis(np.asarray(x, np.float32).astype(ml_dtypes.bfloat16).astype(np.float64), axis, -1)
    blocks = v.reshape(v.shape[:-1] + (-1, 32))
    amax = np.abs(blocks).max(-1, keepdims=True)
    byte = np.maximum(np.where(amax > 0, np.frexp(amax)[1] - 1 + 127, 0) - down, 1)
    scale = np.exp2(byte - 127.0)
    codes = (blocks / scale).astype(np.float32).astype(dtype).astype(np.float64)
    return np.moveaxis((codes * scale).reshape(v.shape), -1, axis)


WIDE = False


def mx_kscale(k):
    if not WIDE:
        return np.ones(k)
    levels = np.array([10, -10, 5, -5, 0])
    a = np.random.permutation(np.resize(levels, k // 512 * 4)).reshape(k // 512, 4)
    idx = np.arange(k)
    return np.exp2(a[idx // 512, idx % 128 // 32])


BF16 = ml_dtypes.bfloat16


def bf(x):
    return np.asarray(x, np.float32).astype(BF16)


def f64(x):
    return np.asarray(x).astype(np.float64)


E2M1 = np.array([0.0, 0.5, 1.0, 1.5, 2.0, 3.0, 4.0, 6.0, -0.0, -0.5, -1.0, -1.5, -2.0, -3.0, -4.0, -6.0])


def pack_weight(w, fmt):
    k, n = w.shape
    w = f64(bf(w)).reshape(k // 32, 32, n)
    amax = np.abs(w).max(1)
    if fmt == "e4m3":
        byte = np.frexp(amax)[1] - 1 + 127 - 7
    else:
        mant, ex = np.frexp(amax / 6.0)
        byte = np.where(mant > 0.5, ex, ex - 1) + 127
    byte = np.clip(np.where(amax > 0, byte, 1), 1, 254)
    scaled = (w * np.exp2(127.0 - byte)[:, None, :]).reshape(k, n).astype(np.float32)
    by_word = np.ascontiguousarray(scaled.reshape(k // 512, 128, 4, n).transpose(0, 1, 3, 2))
    if fmt == "e4m3":
        words = by_word.astype(ml_dtypes.float8_e4m3fn).view(np.uint8)
    else:
        c = by_word.astype(ml_dtypes.float4_e2m1fn).view(np.uint8) & 0xF
        words = c[..., 0::2] | (c[..., 1::2] << 4)
    return np.ascontiguousarray(words), np.ascontiguousarray(byte.astype(np.uint8).reshape(k // 512, 16, n))


def unpack_weight(words, scales, fmt):
    g, p, n, _ = words.shape
    if fmt == "e4m3":
        vals = np.ascontiguousarray(words).view(ml_dtypes.float8_e4m3fn).astype(np.float64)
    else:
        nib = np.empty((g, p, n, 4), np.uint8)
        nib[..., 0::2] = words & 0xF
        nib[..., 1::2] = words >> 4
        vals = E2M1[nib]
    vals = vals * np.repeat(np.exp2(scales.astype(np.float64) - 127.0), 8, axis=1)[..., None]
    return vals.transpose(0, 1, 3, 2).reshape(g * 512, n)


B, C, CI, N = 16, 256, 512, 512
EPS = 1e-5


def setup_inputs():
    s, t = mx_kscale(N), mx_kscale(CI)
    r = np.random.standard_normal
    affinity = bf(r((B, N, N)) * 0.2 * s[None, None, :])
    g_x = bf(r((B, N, CI)) / s[None, :, None] * t[None, None, :])
    w = r((C, CI)) * 1.5 / (0.2 * np.sqrt(N) * np.sqrt(CI)) / t[None, :]
    w_w_words, w_w_scales = pack_weight(np.ascontiguousarray(w.T), "e4m3")
    return {"affinity": affinity,
            "g_x": g_x,
            "w_w_words": w_w_words,
            "w_w_scales": w_w_scales,
            "w_b": bf(r(C) * 0.3),
            "bn_gamma": bf(r(C)),
            "bn_beta": bf(r(C) * 0.5),
            "bn_mean": bf(r(C) * 0.5),
            "bn_var": bf(np.random.uniform(0.5, 1.5, C)),
            "x": bf(r((B, C, N)))}


def reference(affinity, g_x, w_w_words, w_w_scales, w_b, bn_gamma, bn_beta, bn_mean, bn_var, x):
    y = (mxq(f64(affinity), 2, "e4m3") @ mxq(f64(g_x), 1, "e4m3")).transpose(0, 2, 1)
    wy = (unpack_weight(w_w_words, w_w_scales, "e4m3").T @ mxq(y, 1, "e4m3")) + f64(w_b)[None, :, None]
    inv_std = 1.0 / np.sqrt(f64(bn_var) + EPS)
    wy = f64(bn_gamma)[None, :, None] * (wy - f64(bn_mean)[None, :, None]) * inv_std[None, :, None] + f64(bn_beta)[None, :, None]
    return wy + f64(x)

@@ -1,0 +1,223 @@
+from contextlib import ExitStack
+
+import concourse.mybir as mybir
+from concourse.masks import make_identity
+
+F32 = mybir.dt.float32
+BF16 = mybir.dt.bfloat16
+I32 = mybir.dt.int32
+U32 = mybir.dt.uint32
+U8 = mybir.dt.uint8
+FP8X4 = mybir.dt.float8_e4m3fn_x4
+ALU = mybir.AluOpType
+ACT = mybir.ActivationFunctionType
+
+P = 128
+PACK = 4
+B = 16
+N = 512
+CI = 512
+C = 256
+HALVES = C // P
+EPS = 1e-5
+LOOKAHEAD = 6
+
+FLOPS = B * (2 * N * N * CI + 2 * C * CI * N)
+
+
+def tile_sgcam_pb_t_kernel(
+    tc, affinity, g_x, w_w_words, w_w_scales, w_b, bn_gamma, bn_beta, bn_mean, bn_var, x, out
+):
+    nc = tc.nc
+    with ExitStack() as stack:
+        consts = stack.enter_context(tc.tile_pool(name="consts", bufs=1))
+        a_pool = stack.enter_context(tc.tile_pool(name="a_pool", bufs=LOOKAHEAD + 1))
+        g_pool = stack.enter_context(tc.tile_pool(name="g_pool", bufs=LOOKAHEAD + 1))
+        x_pool = stack.enter_context(tc.tile_pool(name="x_pool", bufs=LOOKAHEAD + 2))
+        grouped = stack.enter_context(tc.tile_pool(name="grouped", bufs=2))
+        packed = stack.enter_context(tc.tile_pool(name="packed", bufs=2))
+        res_pool = stack.enter_context(tc.tile_pool(name="res_pool", bufs=4))
+        psum_at = stack.enter_context(tc.psum_pool(name="psum_at", bufs=2))
+        psum_y = stack.enter_context(tc.psum_pool(name="psum_y", bufs=4))
+        psum_wy = stack.enter_context(tc.psum_pool(name="psum_wy", bufs=2))
+
+        live = {}
+
+        ident = consts.tile([P, P], F32)
+        make_identity(nc, ident[:])
+
+        def load_a_g(b):
+            a_sb = a_pool.tile([P, PACK, N], BF16)
+            nc.sync.dma_start(out=a_sb[:], in_=affinity[b].rearrange("(p r) m -> p r m", r=PACK))
+            g_sb = g_pool.tile([P, PACK, CI], BF16)
+            nc.sync.dma_start(
+                out=g_sb[:].rearrange("p (u e) c -> p u (e c)", u=2),
+                in_=g_x[b].rearrange("(u p e) c -> p u (e c)", u=2, e=2),
+            )
+            live["a_sb", b] = a_sb
+            live["g_sb", b] = g_sb
+
+        def load_x(b):
+            x_sb = x_pool.tile([P, HALVES, N], BF16)
+            nc.sync.dma_start(out=x_sb[:], in_=x[b].rearrange("(h p) n -> p h n", h=HALVES))
+            live["x_sb", b] = x_sb
+
+        def transpose_affinity(b):
+            a_words = live["a_sb", b][:].bitcast(F32)
+            a_grouped = grouped.tile([P, N, PACK], BF16, align_bytes=64)
+            a_pairs = a_grouped[:].bitcast(F32).rearrange("q (p r) u -> q p r u", r=PACK)
+            for pair in range(2):
+                at = psum_at.tile([P, 2, 2, P], F32, tag="at")
+                for r in range(2):
+                    for u in range(2):
+                        nc.tensor.transpose(
+                            at[:, r, u, :], a_words[:, 2 * pair + r, P * u : P * (u + 1)], ident[:]
+                        )
+                nc.scalar.copy(
+                    out=a_pairs[:, :, 2 * pair : 2 * pair + 2, :],
+                    in_=at[:].rearrange("q r u p -> q p r u"),
+                )
+            live["a_grouped", b] = a_grouped
+
+        def regroup_values(b):
+            g_grouped = grouped.tile([P, PACK, P, PACK], BF16, align_bytes=64)
+            nc.vector.tensor_copy(
+                out=g_grouped[:].rearrange("q t p j -> q p j t"),
+                in_=live["g_sb", b][:].rearrange("q j (p t) -> q p j t", t=PACK),
+            )
+            live["g_grouped", b] = g_grouped
+
+        def quantise(name, b, flat):
+            codes = packed.tile([P, N], U32, align_bytes=64, tag=name + "_codes", name=name + "_codes")
+            plane = packed.tile([P, N], U8, align_bytes=64, tag=name + "_plane", name=name + "_plane")
+            nc.vector.quantize_mx(out=codes[:].bitcast(FP8X4), scales=plane[:], in_=flat)
+            live[name + "_codes", b] = codes
+            live[name + "_plane", b] = plane
+
+        def aggregate(b):
+            a_codes, a_plane = live["a_codes", b], live["a_plane", b]
+            g_codes, g_plane = live["g_codes", b], live["g_plane", b]
+            y_grouped = grouped.tile([P, N, PACK], BF16, align_bytes=64)
+            for s in range(N // P):
+                n_cols = slice(P * s, P * (s + 1))
+                yt = psum_y.tile([P, PACK, P], F32)
+                for t in range(PACK):
+                    ci_cols = slice(P * t, P * (t + 1))
+                    nc.tensor.matmul_mx(
+                        out=yt[:, t, :],
+                        lhsT=g_codes[:, ci_cols].bitcast(FP8X4),
+                        lhsT_scale=g_plane[:, ci_cols],
+                        rhs=a_codes[:, n_cols].bitcast(FP8X4),
+                        rhs_scale=a_plane[:, n_cols],
+                        start=True,
+                        stop=True,
+                    )
+                nc.scalar.copy(out=y_grouped[:, n_cols, :], in_=yt[:].rearrange("p t n -> p n t"))
+            live["y_grouped", b] = y_grouped
+
+        def project(b):
+            for h in range(HALVES):
+                c_cols = slice(P * h, P * (h + 1))
+                wy = psum_wy.tile([P, N], F32)
+                nc.tensor.matmul_mx(
+                    out=wy[:],
+                    lhsT=w_codes[:, c_cols].bitcast(FP8X4),
+                    lhsT_scale=w_plane[:, c_cols],
+                    rhs=live["y_codes", b][:].bitcast(FP8X4),
+                    rhs_scale=live["y_plane", b][:],
+                    start=True,
+                    stop=True,
+                )
+                live["wy", b, h] = wy
+
+        def shift_residual(b):
+            x_sb = live["x_sb", b]
+            res = res_pool.tile([P, HALVES, N], F32)
+            nc.scalar.activation(
+                out=res[:, 0, :], in_=x_sb[:, 0, :], func=ACT.Identity, bias=shift[:, 0:1], scale=1.0
+            )
+            nc.vector.tensor_scalar_add(out=res[:, 1, :], in0=x_sb[:, 1, :], scalar1=shift[:, 1:2])
+            live["res", b] = res
+
+        def finish(b):
+            res = live["res", b]
+            for h in range(HALVES):
+                nc.vector.scalar_tensor_tensor(
+                    out=res[:, h, :],
+                    in0=live["wy", b, h][:],
+                    scalar=scale[:, h : h + 1],
+                    in1=res[:, h, :],
+                    op0=ALU.mult,
+                    op1=ALU.add,
+                )
+                nc.sync.dma_start(out=out[b, P * h : P * (h + 1), :], in_=res[:, h, :])
+
+        load_a_g(0)
+        w_codes = consts.tile([P, C], U32, align_bytes=64)
+        nc.sync.dma_start(
+            out=w_codes[:].bitcast(I32), in_=w_w_words[0].rearrange("p n t -> p (n t)").bitcast(I32)
+        )
+        w_plane = consts.tile([P, C], U8, align_bytes=64)
+        nc.vector.memset(w_plane[:].bitcast(I32), 0)
+        for quad in range(4):
+            nc.sync.dma_start(
+                out=w_plane[32 * quad : 32 * quad + 4, :].bitcast(I32),
+                in_=w_w_scales[0, 4 * quad : 4 * quad + 4, :].bitcast(I32),
+            )
+        load_x(0)
+        for b in range(1, LOOKAHEAD):
+            load_a_g(b)
+            load_x(b)
+
+        vec_rows = consts.tile([P, P], BF16)
+        nc.vector.memset(vec_rows[:], 0.0)
+        for v, vec in enumerate((w_b, bn_gamma, bn_beta, bn_mean, bn_var)):
+            nc.scalar.dma_start(
+                out=vec_rows[HALVES * v : HALVES * (v + 1), :],
+                in_=vec.rearrange("(h p) -> h p", h=HALVES),
+            )
+
+        transpose_affinity(0)
+        regroup_values(0)
+        quantise("a", 0, live["a_grouped", 0][:].rearrange("q n t -> q (n t)"))
+        quantise("g", 0, live["g_grouped", 0][:].rearrange("q t p j -> q (t p j)"))
+
+        vec_rows_f32 = consts.tile([P, P], F32)
+        nc.vector.tensor_copy(out=vec_rows_f32[:], in_=vec_rows[:])
+        vec_ps = psum_at.tile([P, 2, 2, P], F32, tag="at")
+        nc.tensor.transpose(vec_ps[:, 0, 0, :], vec_rows_f32[:], ident[:])
+        vecs = consts.tile([P, 5, HALVES], F32)
+        nc.vector.tensor_copy(
+            out=vecs[:].rearrange("p v h -> p (v h)"), in_=vec_ps[:, 0, 0, 0 : 5 * HALVES]
+        )
+        bias_c, gamma_c, beta_c, mean_c, var_c = (vecs[:, v, :] for v in range(5))
+        scale = consts.tile([P, HALVES], F32)
+        shift = consts.tile([P, HALVES], F32)
+        nc.vector.tensor_scalar_add(out=scale[:], in0=var_c, scalar1=EPS)
+        nc.scalar.activation(out=scale[:], in_=scale[:], func=ACT.Sqrt)
+        nc.vector.reciprocal(out=scale[:], in_=scale[:])
+        nc.vector.tensor_mul(out=scale[:], in0=scale[:], in1=gamma_c)
+        nc.vector.tensor_sub(out=shift[:], in0=bias_c, in1=mean_c)
+        nc.vector.tensor_mul(out=shift[:], in0=shift[:], in1=scale[:])
+        nc.vector.tensor_add(out=shift[:], in0=shift[:], in1=beta_c)
+
+        for i in range(B + 1):
+            if i + LOOKAHEAD < B:
+                load_a_g(i + LOOKAHEAD)
+                load_x(i + LOOKAHEAD)
+            if i >= 1:
+                quantise("y", i - 1, live["y_grouped", i - 1][:].rearrange("p n t -> p (n t)"))
+            if i + 1 < B:
+                transpose_affinity(i + 1)
+                regroup_values(i + 1)
+            if i < B:
+                aggregate(i)
+            if i >= 1:
+                project(i - 1)
+            if i + 1 < B:
+                quantise("a", i + 1, live["a_grouped", i + 1][:].rearrange("q n t -> q (n t)"))
+                quantise("g", i + 1, live["g_grouped", i + 1][:].rearrange("q t p j -> q (t p j)"))
+            if i < B:
+                shift_residual(i)
+            if i >= 1:
+                finish(i - 1)

@@ -20,7 +20,7 @@ CI = 512
 C = 256
 HALVES = C // P
 EPS = 1e-5
-LOOKAHEAD = 6
+LOOKAHEAD = 5
 
 FLOPS = B * (2 * N * N * CI + 2 * C * CI * N)
 
@@ -30,12 +30,13 @@ def tile_sgcam_pb_t_kernel(
 ):
     nc = tc.nc
     with ExitStack() as stack:
+        stack.enter_context(tc.manual_schedule())
         consts = stack.enter_context(tc.tile_pool(name="consts", bufs=1))
         a_pool = stack.enter_context(tc.tile_pool(name="a_pool", bufs=LOOKAHEAD + 1))
         g_pool = stack.enter_context(tc.tile_pool(name="g_pool", bufs=LOOKAHEAD + 1))
         x_pool = stack.enter_context(tc.tile_pool(name="x_pool", bufs=LOOKAHEAD + 2))
-        grouped = stack.enter_context(tc.tile_pool(name="grouped", bufs=2))
-        packed = stack.enter_context(tc.tile_pool(name="packed", bufs=2))
+        grouped = stack.enter_context(tc.tile_pool(name="grouped", bufs=3))
+        packed = stack.enter_context(tc.tile_pool(name="packed", bufs=3))
         res_pool = stack.enter_context(tc.tile_pool(name="res_pool", bufs=4))
         psum_at = stack.enter_context(tc.psum_pool(name="psum_at", bufs=2))
         psum_y = stack.enter_context(tc.psum_pool(name="psum_y", bufs=4))
@@ -152,22 +153,31 @@ def tile_sgcam_pb_t_kernel(
                 )
                 nc.sync.dma_start(out=out[b, P * h : P * (h + 1), :], in_=res[:, h, :])
 
-        load_a_g(0)
-        w_codes = consts.tile([P, C], U32, align_bytes=64)
-        nc.sync.dma_start(
-            out=w_codes[:].bitcast(I32), in_=w_w_words[0].rearrange("p n t -> p (n t)").bitcast(I32)
-        )
-        w_plane = consts.tile([P, C], U8, align_bytes=64)
-        nc.vector.memset(w_plane[:].bitcast(I32), 0)
-        for quad in range(4):
-            nc.sync.dma_start(
-                out=w_plane[32 * quad : 32 * quad + 4, :].bitcast(I32),
-                in_=w_w_scales[0, 4 * quad : 4 * quad + 4, :].bitcast(I32),
-            )
-        load_x(0)
-        for b in range(1, LOOKAHEAD):
-            load_a_g(b)
-            load_x(b)
+        def issue_loads(j):
+            if 0 <= j < B:
+                load_a_g(j)
+            if 0 <= j - 2 < B:
+                load_x(j - 2)
+
+        def step(i):
+            issue_loads(i + 2 + LOOKAHEAD)
+            if 0 <= i - 2 < B:
+                finish(i - 2)
+            if 0 <= i - 1 < B:
+                quantise("y", i - 1, live["y_grouped", i - 1][:].rearrange("p n t -> p (n t)"))
+            if 0 <= i + 2 < B:
+                transpose_affinity(i + 2)
+            if 0 <= i < B:
+                aggregate(i)
+            if 0 <= i - 1 < B:
+                project(i - 1)
+            if 0 <= i + 1 < B:
+                quantise("a", i + 1, live["a_grouped", i + 1][:].rearrange("q n t -> q (n t)"))
+                quantise("g", i + 1, live["g_grouped", i + 1][:].rearrange("q t p j -> q (t p j)"))
+            if 0 <= i + 2 < B:
+                regroup_values(i + 2)
+            if 0 <= i - 1 < B:
+                shift_residual(i - 1)
 
         vec_rows = consts.tile([P, P], BF16)
         nc.vector.memset(vec_rows[:], 0.0)
@@ -177,10 +187,21 @@ def tile_sgcam_pb_t_kernel(
                 in_=vec.rearrange("(h p) -> h p", h=HALVES),
             )
 
-        transpose_affinity(0)
-        regroup_values(0)
-        quantise("a", 0, live["a_grouped", 0][:].rearrange("q n t -> q (n t)"))
-        quantise("g", 0, live["g_grouped", 0][:].rearrange("q t p j -> q (t p j)"))
+        w_codes = consts.tile([P, C], U32, align_bytes=64)
+        w_plane = consts.tile([P, C], U8, align_bytes=64)
+        nc.vector.memset(w_plane[:].bitcast(I32), 0)
+        issue_loads(0)
+        issue_loads(1)
+        nc.sync.dma_start(
+            out=w_codes[:].bitcast(I32), in_=w_w_words[0].rearrange("p n t -> p (n t)").bitcast(I32)
+        )
+        for quad in range(4):
+            nc.sync.dma_start(
+                out=w_plane[32 * quad : 32 * quad + 4, :].bitcast(I32),
+                in_=w_w_scales[0, 4 * quad : 4 * quad + 4, :].bitcast(I32),
+            )
+        for j in range(2, LOOKAHEAD):
+            issue_loads(j)
 
         vec_rows_f32 = consts.tile([P, P], F32)
         nc.vector.tensor_copy(out=vec_rows_f32[:], in_=vec_rows[:])
@@ -195,29 +216,15 @@ def tile_sgcam_pb_t_kernel(
         shift = consts.tile([P, HALVES], F32)
         nc.vector.tensor_scalar_add(out=scale[:], in0=var_c, scalar1=EPS)
         nc.scalar.activation(out=scale[:], in_=scale[:], func=ACT.Sqrt)
+
+        step(-2)
+        step(-1)
+
         nc.vector.reciprocal(out=scale[:], in_=scale[:])
         nc.vector.tensor_mul(out=scale[:], in0=scale[:], in1=gamma_c)
         nc.vector.tensor_sub(out=shift[:], in0=bias_c, in1=mean_c)
         nc.vector.tensor_mul(out=shift[:], in0=shift[:], in1=scale[:])
         nc.vector.tensor_add(out=shift[:], in0=shift[:], in1=beta_c)
 
-        for i in range(B + 1):
-            if i + LOOKAHEAD < B:
-                load_a_g(i + LOOKAHEAD)
-                load_x(i + LOOKAHEAD)
-            if i >= 1:
-                quantise("y", i - 1, live["y_grouped", i - 1][:].rearrange("p n t -> p (n t)"))
-            if i + 1 < B:
-                transpose_affinity(i + 1)
-                regroup_values(i + 1)
-            if i < B:
-                aggregate(i)
-            if i >= 1:
-                project(i - 1)
-            if i + 1 < B:
-                quantise("a", i + 1, live["a_grouped", i + 1][:].rearrange("q n t -> q (n t)"))
-                quantise("g", i + 1, live["g_grouped", i + 1][:].rearrange("q t p j -> q (t p j)"))
-            if i < B:
-                shift_residual(i)
-            if i >= 1:
-                finish(i - 1)
+        for i in range(B + 2):
+            step(i)

@@ -134,10 +134,15 @@ def tile_sgcam_pb_t_kernel(
         def shift_residual(b):
             x_sb = live["x_sb", b]
             res = res_pool.tile([P, HALVES, N], F32)
-            nc.scalar.activation(
-                out=res[:, 0, :], in_=x_sb[:, 0, :], func=ACT.Identity, bias=shift[:, 0:1], scale=1.0
-            )
-            nc.vector.tensor_scalar_add(out=res[:, 1, :], in0=x_sb[:, 1, :], scalar1=shift[:, 1:2])
+            for h in range(HALVES):
+                nc.gpsimd.tensor_scalar(
+                    out=res[:, h, :],
+                    in0=x_sb[:, h, :],
+                    scalar1=1.0,
+                    scalar2=shift[:, h : h + 1],
+                    op0=ALU.mult,
+                    op1=ALU.add,
+                )
             live["res", b] = res
 
         def finish(b):

@@ -34,7 +34,7 @@ def tile_sgcam_pb_t_kernel(
         consts = stack.enter_context(tc.tile_pool(name="consts", bufs=1))
         a_pool = stack.enter_context(tc.tile_pool(name="a_pool", bufs=LOOKAHEAD + 1))
         g_pool = stack.enter_context(tc.tile_pool(name="g_pool", bufs=LOOKAHEAD + 1))
-        x_pool = stack.enter_context(tc.tile_pool(name="x_pool", bufs=LOOKAHEAD + 2))
+        x_pool = stack.enter_context(tc.tile_pool(name="x_pool", bufs=LOOKAHEAD + 3))
         grouped = stack.enter_context(tc.tile_pool(name="grouped", bufs=3))
         packed = stack.enter_context(tc.tile_pool(name="packed", bufs=3))
         res_pool = stack.enter_context(tc.tile_pool(name="res_pool", bufs=4))
@@ -131,32 +131,22 @@ def tile_sgcam_pb_t_kernel(
                 )
                 live["wy", b, h] = wy
 
-        def shift_residual(b):
-            x_sb = live["x_sb", b]
+        def scale_and_shift(b):
             res = res_pool.tile([P, HALVES, N], F32)
             for h in range(HALVES):
-                nc.gpsimd.tensor_scalar(
+                nc.scalar.activation(
                     out=res[:, h, :],
-                    in0=x_sb[:, h, :],
-                    scalar1=1.0,
-                    scalar2=shift[:, h : h + 1],
-                    op0=ALU.mult,
-                    op1=ALU.add,
+                    in_=live["wy", b, h][:],
+                    func=ACT.Identity,
+                    bias=shift[:, h : h + 1],
+                    scale=scale[:, h : h + 1],
                 )
             live["res", b] = res
 
-        def finish(b):
+        def add_residual_and_store(b):
             res = live["res", b]
-            for h in range(HALVES):
-                nc.vector.scalar_tensor_tensor(
-                    out=res[:, h, :],
-                    in0=live["wy", b, h][:],
-                    scalar=scale[:, h : h + 1],
-                    in1=res[:, h, :],
-                    op0=ALU.mult,
-                    op1=ALU.add,
-                )
-                nc.sync.dma_start(out=out[b, P * h : P * (h + 1), :], in_=res[:, h, :])
+            nc.vector.tensor_add(out=res[:], in0=res[:], in1=live["x_sb", b][:])
+            nc.sync.dma_start(out=out[b].rearrange("(h p) n -> p h n", h=HALVES), in_=res[:])
 
         def issue_loads(j):
             if 0 <= j < B:
@@ -167,7 +157,7 @@ def tile_sgcam_pb_t_kernel(
         def step(i):
             issue_loads(i + 2 + LOOKAHEAD)
             if 0 <= i - 2 < B:
-                finish(i - 2)
+                add_residual_and_store(i - 2)
             if 0 <= i - 1 < B:
                 quantise("y", i - 1, live["y_grouped", i - 1][:].rearrange("p n t -> p (n t)"))
             if 0 <= i + 2 < B:
@@ -176,13 +166,12 @@ def tile_sgcam_pb_t_kernel(
                 aggregate(i)
             if 0 <= i - 1 < B:
                 project(i - 1)
+                scale_and_shift(i - 1)
             if 0 <= i + 1 < B:
                 quantise("a", i + 1, live["a_grouped", i + 1][:].rearrange("q n t -> q (n t)"))
                 quantise("g", i + 1, live["g_grouped", i + 1][:].rearrange("q t p j -> q (t p j)"))
             if 0 <= i + 2 < B:
                 regroup_values(i + 2)
-            if 0 <= i - 1 < B:
-                shift_residual(i - 1)
 
         vec_rows = consts.tile([P, P], BF16)
         nc.vector.memset(vec_rows[:], 0.0)

from contextlib import ExitStack

import concourse.mybir as mybir
from concourse.masks import make_identity

F32 = mybir.dt.float32
BF16 = mybir.dt.bfloat16
I32 = mybir.dt.int32
U32 = mybir.dt.uint32
U8 = mybir.dt.uint8
FP8X4 = mybir.dt.float8_e4m3fn_x4
ALU = mybir.AluOpType
ACT = mybir.ActivationFunctionType

P = 128
PACK = 4
B = 16
N = 512
CI = 512
C = 256
HALVES = C // P
EPS = 1e-5
LOOKAHEAD = 5

FLOPS = B * (2 * N * N * CI + 2 * C * CI * N)


def tile_sgcam_pb_t_kernel(
    tc, affinity, g_x, w_w_words, w_w_scales, w_b, bn_gamma, bn_beta, bn_mean, bn_var, x, out
):
    nc = tc.nc
    with ExitStack() as stack:
        stack.enter_context(tc.manual_schedule())
        consts = stack.enter_context(tc.tile_pool(name="consts", bufs=1))
        a_pool = stack.enter_context(tc.tile_pool(name="a_pool", bufs=LOOKAHEAD + 1))
        g_pool = stack.enter_context(tc.tile_pool(name="g_pool", bufs=LOOKAHEAD + 1))
        x_pool = stack.enter_context(tc.tile_pool(name="x_pool", bufs=LOOKAHEAD + 3))
        grouped = stack.enter_context(tc.tile_pool(name="grouped", bufs=3))
        packed = stack.enter_context(tc.tile_pool(name="packed", bufs=3))
        res_pool = stack.enter_context(tc.tile_pool(name="res_pool", bufs=4))
        psum_at = stack.enter_context(tc.psum_pool(name="psum_at", bufs=2))
        psum_y = stack.enter_context(tc.psum_pool(name="psum_y", bufs=4))
        psum_wy = stack.enter_context(tc.psum_pool(name="psum_wy", bufs=2))

        live = {}

        ident = consts.tile([P, P], F32)
        make_identity(nc, ident[:])

        def load_a_g(b):
            a_sb = a_pool.tile([P, PACK, N], BF16)
            nc.sync.dma_start(out=a_sb[:], in_=affinity[b].rearrange("(p r) m -> p r m", r=PACK))
            g_sb = g_pool.tile([P, PACK, CI], BF16)
            nc.sync.dma_start(
                out=g_sb[:].rearrange("p (u e) c -> p u (e c)", u=2),
                in_=g_x[b].rearrange("(u p e) c -> p u (e c)", u=2, e=2),
            )
            live["a_sb", b] = a_sb
            live["g_sb", b] = g_sb

        def load_x(b):
            x_sb = x_pool.tile([P, HALVES, N], BF16)
            nc.sync.dma_start(out=x_sb[:], in_=x[b].rearrange("(h p) n -> p h n", h=HALVES))
            live["x_sb", b] = x_sb

        def transpose_affinity(b):
            a_words = live["a_sb", b][:].bitcast(F32)
            a_grouped = grouped.tile([P, N, PACK], BF16, align_bytes=64)
            a_pairs = a_grouped[:].bitcast(F32).rearrange("q (p r) u -> q p r u", r=PACK)
            for pair in range(2):
                at = psum_at.tile([P, 2, 2, P], F32, tag="at")
                for r in range(2):
                    for u in range(2):
                        nc.tensor.transpose(
                            at[:, r, u, :], a_words[:, 2 * pair + r, P * u : P * (u + 1)], ident[:]
                        )
                nc.scalar.copy(
                    out=a_pairs[:, :, 2 * pair : 2 * pair + 2, :],
                    in_=at[:].rearrange("q r u p -> q p r u"),
                )
            live["a_grouped", b] = a_grouped

        def regroup_values(b):
            g_grouped = grouped.tile([P, PACK, P, PACK], BF16, align_bytes=64)
            nc.vector.tensor_copy(
                out=g_grouped[:].rearrange("q t p j -> q p j t"),
                in_=live["g_sb", b][:].rearrange("q j (p t) -> q p j t", t=PACK),
            )
            live["g_grouped", b] = g_grouped

        def quantise(name, b, flat):
            codes = packed.tile([P, N], U32, align_bytes=64, tag=name + "_codes", name=name + "_codes")
            plane = packed.tile([P, N], U8, align_bytes=64, tag=name + "_plane", name=name + "_plane")
            nc.vector.quantize_mx(out=codes[:].bitcast(FP8X4), scales=plane[:], in_=flat)
            live[name + "_codes", b] = codes
            live[name + "_plane", b] = plane

        def aggregate(b):
            a_codes, a_plane = live["a_codes", b], live["a_plane", b]
            g_codes, g_plane = live["g_codes", b], live["g_plane", b]
            y_grouped = grouped.tile([P, N, PACK], BF16, align_bytes=64)
            for s in range(N // P):
                n_cols = slice(P * s, P * (s + 1))
                yt = psum_y.tile([P, PACK, P], F32)
                for t in range(PACK):
                    ci_cols = slice(P * t, P * (t + 1))
                    nc.tensor.matmul_mx(
                        out=yt[:, t, :],
                        lhsT=g_codes[:, ci_cols].bitcast(FP8X4),
                        lhsT_scale=g_plane[:, ci_cols],
                        rhs=a_codes[:, n_cols].bitcast(FP8X4),
                        rhs_scale=a_plane[:, n_cols],
                        start=True,
                        stop=True,
                    )
                nc.scalar.copy(out=y_grouped[:, n_cols, :], in_=yt[:].rearrange("p t n -> p n t"))
            live["y_grouped", b] = y_grouped

        def project(b):
            for h in range(HALVES):
                c_cols = slice(P * h, P * (h + 1))
                wy = psum_wy.tile([P, N], F32)
                nc.tensor.matmul_mx(
                    out=wy[:],
                    lhsT=w_codes[:, c_cols].bitcast(FP8X4),
                    lhsT_scale=w_plane[:, c_cols],
                    rhs=live["y_codes", b][:].bitcast(FP8X4),
                    rhs_scale=live["y_plane", b][:],
                    start=True,
                    stop=True,
                )
                live["wy", b, h] = wy

        def scale_and_shift(b):
            res = res_pool.tile([P, HALVES, N], F32)
            for h in range(HALVES):
                nc.scalar.activation(
                    out=res[:, h, :],
                    in_=live["wy", b, h][:],
                    func=ACT.Identity,
                    bias=shift[:, h : h + 1],
                    scale=scale[:, h : h + 1],
                )
            live["res", b] = res

        def add_residual_and_store(b):
            res = live["res", b]
            nc.vector.tensor_add(out=res[:], in0=res[:], in1=live["x_sb", b][:])
            nc.sync.dma_start(out=out[b].rearrange("(h p) n -> p h n", h=HALVES), in_=res[:])

        def issue_loads(j):
            if 0 <= j < B:
                load_a_g(j)
            if 0 <= j - 2 < B:
                load_x(j - 2)

        def step(i):
            issue_loads(i + 2 + LOOKAHEAD)
            if 0 <= i - 2 < B:
                add_residual_and_store(i - 2)
            if 0 <= i - 1 < B:
                quantise("y", i - 1, live["y_grouped", i - 1][:].rearrange("p n t -> p (n t)"))
            if 0 <= i + 2 < B:
                transpose_affinity(i + 2)
            if 0 <= i < B:
                aggregate(i)
            if 0 <= i - 1 < B:
                project(i - 1)
                scale_and_shift(i - 1)
            if 0 <= i + 1 < B:
                quantise("a", i + 1, live["a_grouped", i + 1][:].rearrange("q n t -> q (n t)"))
                quantise("g", i + 1, live["g_grouped", i + 1][:].rearrange("q t p j -> q (t p j)"))
            if 0 <= i + 2 < B:
                regroup_values(i + 2)

        vec_rows = consts.tile([P, P], BF16)
        nc.vector.memset(vec_rows[:], 0.0)
        for v, vec in enumerate((w_b, bn_gamma, bn_beta, bn_mean, bn_var)):
            nc.scalar.dma_start(
                out=vec_rows[HALVES * v : HALVES * (v + 1), :],
                in_=vec.rearrange("(h p) -> h p", h=HALVES),
            )

        w_codes = consts.tile([P, C], U32, align_bytes=64)
        w_plane = consts.tile([P, C], U8, align_bytes=64)
        nc.vector.memset(w_plane[:].bitcast(I32), 0)
        issue_loads(0)
        issue_loads(1)
        nc.sync.dma_start(
            out=w_codes[:].bitcast(I32), in_=w_w_words[0].rearrange("p n t -> p (n t)").bitcast(I32)
        )
        for quad in range(4):
            nc.sync.dma_start(
                out=w_plane[32 * quad : 32 * quad + 4, :].bitcast(I32),
                in_=w_w_scales[0, 4 * quad : 4 * quad + 4, :].bitcast(I32),
            )
        for j in range(2, LOOKAHEAD):
            issue_loads(j)

        vec_rows_f32 = consts.tile([P, P], F32)
        nc.vector.tensor_copy(out=vec_rows_f32[:], in_=vec_rows[:])
        vec_ps = psum_at.tile([P, 2, 2, P], F32, tag="at")
        nc.tensor.transpose(vec_ps[:, 0, 0, :], vec_rows_f32[:], ident[:])
        vecs = consts.tile([P, 5, HALVES], F32)
        nc.vector.tensor_copy(
            out=vecs[:].rearrange("p v h -> p (v h)"), in_=vec_ps[:, 0, 0, 0 : 5 * HALVES]
        )
        bias_c, gamma_c, beta_c, mean_c, var_c = (vecs[:, v, :] for v in range(5))
        scale = consts.tile([P, HALVES], F32)
        shift = consts.tile([P, HALVES], F32)
        nc.vector.tensor_scalar_add(out=scale[:], in0=var_c, scalar1=EPS)
        nc.scalar.activation(out=scale[:], in_=scale[:], func=ACT.Sqrt)

        step(-2)
        step(-1)

        nc.vector.reciprocal(out=scale[:], in_=scale[:])
        nc.vector.tensor_mul(out=scale[:], in0=scale[:], in1=gamma_c)
        nc.vector.tensor_sub(out=shift[:], in0=bias_c, in1=mean_c)
        nc.vector.tensor_mul(out=shift[:], in0=shift[:], in1=scale[:])
        nc.vector.tensor_add(out=shift[:], in0=shift[:], in1=beta_c)

        for i in range(B + 2):
            step(i)
